import numpy as np
import ml_dtypes


def mxq(x, axis, fmt="e4m3"):
    dtype, down = {"e4m3": (ml_dtypes.float8_e4m3fn, 7), "e5m2": (ml_dtypes.float8_e5m2, 14)}[fmt]
    v = np.moveaxis(np.asarray(x, np.float32).astype(ml_dtypes.bfloat16).astype(np.float64), axis, -1)
    blocks = v.reshape(v.shape[:-1] + (-1, 32))
    amax = np.abs(blocks).max(-1, keepdims=True)
    byte = np.maximum(np.where(amax > 0, np.frexp(amax)[1] - 1 + 127, 0) - down, 1)
    scale = np.exp2(byte - 127.0)
    codes = (blocks / scale).astype(np.float32).astype(dtype).astype(np.float64)
    return np.moveaxis((codes * scale).reshape(v.shape), -1, axis)


WIDE = False


def mx_kscale(k):
    if not WIDE:
        return np.ones(k)
    levels = np.array([10, -10, 5, -5, 0])
    a = np.random.permutation(np.resize(levels, k // 512 * 4)).reshape(k // 512, 4)
    idx = np.arange(k)
    return np.exp2(a[idx // 512, idx % 128 // 32])


BF16 = ml_dtypes.bfloat16


def bf(x):
    return np.asarray(x, np.float32).astype(BF16)


def f64(x):
    return np.asarray(x).astype(np.float64)


B, S, D, H, DH, DR, DKV, DQ = 1, 1024, 2048, 16, 128, 64, 512, 1024
HALF = DR // 2


def rope(t, cos, sin):
    t1, t2 = t[..., 0::2], t[..., 1::2]
    c = cos[None, :, None, :]
    s = sin[None, :, None, :]
    return np.stack([t1 * c - t2 * s, t1 * s + t2 * c], axis=-1).reshape(t.shape)


def setup_inputs():
    s, t = mx_kscale(D), mx_kscale(DKV)
    ang = np.random.uniform(0.0, 2.0 * np.pi, (S, HALF))
    return {"x": bf(np.random.standard_normal((B, S, D)) * s),
            "W_kv_down": bf(np.random.standard_normal((D, DKV)) / np.sqrt(D) / s[:, None] * t),
            "W_k_up": bf(np.random.standard_normal((DKV, H * DH)) / np.sqrt(DKV) / t[:, None]),
            "W_v_up": bf(np.random.standard_normal((DKV, H * DH)) / np.sqrt(DKV) / t[:, None]),
            "W_k_rope": bf(np.random.standard_normal((D, H * DR)) / np.sqrt(D) / s[:, None]),
            "rope_cos": bf(np.cos(ang)), "rope_sin": bf(np.sin(ang))}


def reference(x, W_kv_down, W_k_up, W_v_up, W_k_rope, rope_cos, rope_sin):
    xq = mxq(f64(x), 2, "e4m3")
    down_kv = xq @ mxq(f64(W_kv_down), 0, "e4m3")
    dkv = mxq(down_kv, 2, "e4m3")
    k_c = (dkv @ mxq(f64(W_k_up), 0, "e4m3")).reshape(B, S, H, DH)
    v = (dkv @ mxq(f64(W_v_up), 0, "e4m3")).reshape(B, S, H, DH)
    k_r = (xq @ mxq(f64(W_k_rope), 0, "e4m3")).reshape(B, S, H, DR)
    k_r = rope(k_r, f64(rope_cos), f64(rope_sin))
    k = np.concatenate([k_c, k_r], axis=-1).transpose(0, 2, 1, 3)
    return k, v.transpose(0, 2, 1, 3)

@@ -1,0 +1,327 @@
+from contextlib import ExitStack
+
+import concourse.mybir as mybir
+from concourse.masks import make_identity
+
+F32 = mybir.dt.float32
+BF16 = mybir.dt.bfloat16
+U32 = mybir.dt.uint32
+U8 = mybir.dt.uint8
+FP8X4 = mybir.dt.float8_e4m3fn_x4
+MULT = mybir.AluOpType.mult
+ADD = mybir.AluOpType.add
+
+P = 128
+PACK = 4
+K_PASS = P * PACK
+BANK = 512
+
+TOKENS = 1024
+MODEL = 2048
+LATENT = 512
+HEADS = 16
+HEAD = 128
+ROT = 64
+PAIRS = ROT // 2
+
+CHUNKS = TOKENS // P
+PASSES = MODEL // K_PASS
+GROUP = BANK // HEAD
+GROUPS = HEADS // GROUP
+ROT_COLS = GROUP * ROT
+
+FLOPS = 2 * TOKENS * (MODEL * LATENT + 2 * LATENT * HEADS * HEAD + MODEL * HEADS * ROT)
+
+
+def tile_multiheadlatentattention_pb_kernel(
+    tc, x, W_kv_down, W_k_up, W_v_up, W_k_rope, rope_cos, rope_sin, out_0, out_1
+):
+    nc = tc.nc
+    with ExitStack() as ctx:
+        const = ctx.enter_context(tc.tile_pool(name="const", bufs=1))
+        keep = ctx.enter_context(tc.tile_pool(name="keep", bufs=1))
+        raw_pool = ctx.enter_context(tc.tile_pool(name="raw", bufs=6))
+        grouped_pool = ctx.enter_context(tc.tile_pool(name="grouped", bufs=4))
+        rot_pool = ctx.enter_context(tc.tile_pool(name="rot", bufs=2))
+        stage_pool = ctx.enter_context(tc.tile_pool(name="stage", bufs=3))
+        psum = ctx.enter_context(tc.psum_pool(name="psum", bufs=8))
+        ctx.enter_context(tc.manual_schedule())
+
+        x_codes = keep.tile([P, CHUNKS, PASSES, P], U32, align_bytes=64)
+        x_scales = keep.tile([P, CHUNKS, PASSES, P], U8, align_bytes=64)
+        down_codes = keep.tile([P, PASSES, LATENT], U32, align_bytes=64)
+        down_scales = keep.tile([P, PASSES, LATENT], U8, align_bytes=64)
+        rope_codes = keep.tile([P, PASSES, HEADS * ROT], U32, align_bytes=64)
+        rope_scales = keep.tile([P, PASSES, HEADS * ROT], U8, align_bytes=64)
+        latent_codes = keep.tile([P, CHUNKS, P], U32, align_bytes=64)
+        latent_scales = keep.tile([P, CHUNKS, P], U8, align_bytes=64)
+        k_up_codes = keep.tile([P, HEADS * HEAD], U32, align_bytes=64)
+        k_up_scales = keep.tile([P, HEADS * HEAD], U8, align_bytes=64)
+        v_up_codes = keep.tile([P, HEADS * HEAD], U32, align_bytes=64)
+        v_up_scales = keep.tile([P, HEADS * HEAD], U8, align_bytes=64)
+
+        def load(shape, source):
+            raw = raw_pool.tile(shape, BF16, tag="raw", name="raw")
+            nc.sync.dma_start(out=raw[:], in_=source)
+            return raw
+
+        x_view = x.rearrange("b (p j) k -> p (b j) k", j=CHUNKS)
+
+        def load_x(c):
+            return load([P, 2, MODEL], x_view[:, 2 * c : 2 * c + 2, :])
+
+        down_view = W_kv_down.rearrange("(s q e) n -> q s (e n)", q=P, e=2)
+        rope_view = W_k_rope.rearrange("(s q e) n -> q s (e n)", q=P, e=2)
+
+        def load_down(c):
+            return load([P, 4, 2 * LATENT], down_view[:, 4 * c : 4 * c + 4, :])
+
+        def load_rope(g):
+            return load([P, 2, 2 * HEADS * ROT], rope_view[:, 2 * g : 2 * g + 2, :])
+
+        def load_up(weight, c):
+            view = weight.rearrange("(t p) n -> p t n", p=P)
+            return load([P, PACK, 2 * BANK], view[:, :, 2 * BANK * c : 2 * BANK * (c + 1)])
+
+        down_raw = [load_down(0), load_down(1)]
+        x_raw = [load_x(0)]
+        v_up_raw = [load_up(W_v_up, 0)]
+        rope_raw = []
+        for c in range(1, CHUNKS // 2):
+            x_raw.append(load_x(c))
+            rope_raw.append(load_rope(c - 1))
+        rope_raw.append(load_rope(PASSES - 1))
+        v_up_raw.append(load_up(W_v_up, 1))
+        k_up_raw = [load_up(W_k_up, 0), load_up(W_k_up, 1)]
+
+        ident = const.tile([P, P], F32)
+        make_identity(nc, ident[:])
+        cos_bf = const.tile([P, CHUNKS, PAIRS], BF16)
+        sin_bf = const.tile([P, CHUNKS, PAIRS], BF16)
+        nc.scalar.dma_start(out=cos_bf[:], in_=rope_cos.rearrange("(p j) i -> p j i", j=CHUNKS))
+        nc.scalar.dma_start(out=sin_bf[:], in_=rope_sin.rearrange("(p j) i -> p j i", j=CHUNKS))
+
+        def regroup(copy, rows):
+            grouped = grouped_pool.tile([P, BANK, PACK], BF16, tag="grouped", name="grouped", align_bytes=64)
+            copy(
+                out=grouped[:].rearrange("p (c i) t -> p c t i", i=4),
+                in_=rows.rearrange("p t (c i) -> p c t i", i=4),
+            )
+            return grouped
+
+        def quantise(grouped, codes, scales):
+            nc.vector.quantize_mx(
+                out=codes.bitcast(FP8X4), scales=scales, in_=grouped[:].rearrange("p n t -> p (n t)")
+            )
+
+        def prepare(first, second, second_copy=nc.vector.tensor_copy):
+            grouped_first = regroup(nc.vector.tensor_copy, first[0])
+            grouped_second = regroup(second_copy, second[0])
+            quantise(grouped_first, first[1], first[2])
+            quantise(grouped_second, second[1], second[2])
+
+        def prepare_down(c):
+            rows = down_raw[c][:].rearrange("p s (e n) -> p (s e) n", e=2)
+            halves = [
+                (rows[:, PACK * i : PACK * i + PACK, :], down_codes[:, 2 * c + i, :], down_scales[:, 2 * c + i, :])
+                for i in range(2)
+            ]
+            prepare(halves[0], halves[1], second_copy=nc.scalar.copy)
+
+        def prepare_rope(g):
+            rows = rope_raw[g][:].rearrange("p s (e n) -> p (s e) n", e=2)
+            halves = [
+                (rows[:, :, BANK * i : BANK * i + BANK], rope_codes[:, g, BANK * i : BANK * i + BANK],
+                 rope_scales[:, g, BANK * i : BANK * i + BANK])
+                for i in range(2)
+            ]
+            prepare(halves[0], halves[1])
+
+        def prepare_up(raw, codes, scales, c):
+            halves = [
+                (raw[c][:, :, BANK * i : BANK * i + BANK], codes[:, BANK * (2 * c + i) : BANK * (2 * c + i + 1)],
+                 scales[:, BANK * (2 * c + i) : BANK * (2 * c + i + 1)])
+                for i in range(2)
+            ]
+            prepare(halves[0], halves[1])
+
+        def flip(j):
+            words = x_raw[j // 2][:, j % 2, :].bitcast(F32)
+            x_grouped = grouped_pool.tile([P, PASSES * P * PACK], BF16, tag="grouped", name="x_grouped", align_bytes=64)
+            x_grouped_words = x_grouped[:].bitcast(F32).rearrange("p (g r u) -> p g r u", g=PASSES, u=2)
+            for b in range(2):
+                flipped = psum.tile([P, BANK], F32, tag="bank", name="flipped")
+                for w in range(4):
+                    first = P * (4 * b + w)
+                    nc.tensor.transpose(flipped[:, P * w : P * w + P], words[:, first : first + P], ident[:])
+                nc.scalar.copy(
+                    out=x_grouped_words[:, 2 * b : 2 * b + 2, :, :],
+                    in_=flipped[:].rearrange("p (g u r) -> p g r u", g=2, u=2),
+                )
+            return x_grouped
+
+        def quantise_x(j, x_grouped):
+            nc.vector.quantize_mx(
+                out=x_codes[:, j, :, :].rearrange("p g r -> p (g r)").bitcast(FP8X4),
+                scales=x_scales[:, j, :, :].rearrange("p g r -> p (g r)"),
+                in_=x_grouped[:],
+            )
+
+        def project_down(j):
+            latent = psum.tile([P, BANK], F32, tag="bank", name="latent")
+            for t in range(PACK):
+                for g in range(PASSES):
+                    nc.tensor.matmul_mx(
+                        out=latent[:, P * t : P * t + P],
+                        lhsT=down_codes[:, g, P * t : P * t + P].bitcast(FP8X4),
+                        lhsT_scale=down_scales[:, g, P * t : P * t + P],
+                        rhs=x_codes[:, j, g, :].bitcast(FP8X4),
+                        rhs_scale=x_scales[:, j, g, :],
+                        start=(g == 0),
+                        stop=(g == PASSES - 1),
+                    )
+            latent_grouped = grouped_pool.tile([P, P, PACK], BF16, tag="latent_grouped", name="latent_grouped", align_bytes=64)
+            nc.scalar.copy(out=latent_grouped[:], in_=latent[:].rearrange("p (t r) -> p r t", t=PACK))
+            return latent_grouped
+
+        def quantise_latent(j, latent_grouped):
+            nc.vector.quantize_mx(
+                out=latent_codes[:, j, :].bitcast(FP8X4),
+                scales=latent_scales[:, j, :],
+                in_=latent_grouped[:].rearrange("p r t -> p (r t)"),
+            )
+
+        def project_up(codes, scales, n, j, target):
+            cols = slice(BANK * n, BANK * n + BANK)
+            acc = psum.tile([P, BANK], F32, tag="bank", name="acc")
+            nc.tensor.matmul_mx(
+                out=acc[:],
+                lhsT=latent_codes[:, j, :].bitcast(FP8X4),
+                lhsT_scale=latent_scales[:, j, :],
+                rhs=codes[:, cols].bitcast(FP8X4),
+                rhs_scale=scales[:, cols],
+                start=True,
+                stop=True,
+            )
+            nc.scalar.copy(out=target, in_=acc[:].rearrange("p (h d) -> p h d", h=GROUP))
+
+        values_view = out_1.rearrange("b h (p j) d -> p (b h) j d", j=CHUNKS)
+        keys_view = out_0.rearrange("b h (p j) d -> p (b h) j d", j=CHUNKS)
+
+        def new_values_stage():
+            return stage_pool.tile([P, GROUP, CHUNKS, HEAD], F32, tag="stage", name="stage_v")
+
+        def values(n, j, stage):
+            project_up(v_up_codes, v_up_scales, n, j, stage[:, :, j, :])
+
+        def store_values(n, stage):
+            nc.sync.dma_start(out=values_view[:, GROUP * n : GROUP * n + GROUP, :, :], in_=stage[:])
+
+        def rotary(n, j0):
+            rot_cols = slice(ROT_COLS * n, ROT_COLS * n + ROT_COLS)
+            acc_r = psum.tile([P, BANK], F32, tag="bank", name="acc_r")
+            for c in range(2):
+                for g in range(PASSES):
+                    nc.tensor.matmul_mx(
+                        out=acc_r[:, ROT_COLS * c : ROT_COLS * c + ROT_COLS],
+                        lhsT=x_codes[:, j0 + c, g, :].bitcast(FP8X4),
+                        lhsT_scale=x_scales[:, j0 + c, g, :],
+                        rhs=rope_codes[:, g, rot_cols].bitcast(FP8X4),
+                        rhs_scale=rope_scales[:, g, rot_cols],
+                        start=(g == 0),
+                        stop=(g == PASSES - 1),
+                    )
+            return acc_r
+
+        def rotate(acc_r, j0, stage):
+            two = slice(j0, j0 + 2)
+            by_feature = acc_r[:].rearrange("p (c h f) -> p c h f", c=2, h=GROUP)
+            by_pair = acc_r[:].rearrange("p (c h i e) -> p c h i e", c=2, h=GROUP, e=2)
+            with_cos = rot_pool.tile([P, 2, GROUP, PAIRS, 2], F32, tag="with_cos", name="with_cos")
+            nc.vector.tensor_tensor(
+                out=with_cos[:].rearrange("p c h i e -> p c h (i e)"),
+                in0=by_feature,
+                in1=cos_twice[:, two, :, :].rearrange("p c i e -> p c (i e)").unsqueeze(2).to_broadcast([P, 2, GROUP, ROT]),
+                op=MULT,
+            )
+            with_sin = rot_pool.tile([P, 2, 2, GROUP, PAIRS], F32, tag="with_sin", name="with_sin")
+            nc.vector.tensor_tensor(
+                out=with_sin[:, 0, :, :, :],
+                in0=by_pair[:, :, :, :, 1],
+                in1=sin_minus[:, two, :].unsqueeze(2).to_broadcast([P, 2, GROUP, PAIRS]),
+                op=MULT,
+            )
+            nc.vector.tensor_tensor(
+                out=with_sin[:, 1, :, :, :],
+                in0=by_pair[:, :, :, :, 0],
+                in1=sin_plus[:, two, :].unsqueeze(2).to_broadcast([P, 2, GROUP, PAIRS]),
+                op=MULT,
+            )
+            nc.gpsimd.tensor_tensor(
+                out=stage[:, :, two, HEAD : HEAD + ROT].rearrange("p h c (i e) -> p c h i e", e=2),
+                in0=with_cos[:],
+                in1=with_sin[:].rearrange("p e c h i -> p c h i e"),
+                op=ADD,
+            )
+
+        prepare_down(0)
+        prepare_down(1)
+
+        cos_twice = const.tile([P, CHUNKS, PAIRS, 2], F32)
+        nc.vector.tensor_copy(
+            out=cos_twice[:], in_=cos_bf[:].unsqueeze(3).to_broadcast([P, CHUNKS, PAIRS, 2])
+        )
+        sin_plus = const.tile([P, CHUNKS, PAIRS], F32)
+        nc.vector.tensor_copy(out=sin_plus[:], in_=sin_bf[:])
+        sin_minus = const.tile([P, CHUNKS, PAIRS], F32)
+        nc.vector.tensor_scalar_mul(out=sin_minus[:], in0=sin_bf[:], scalar1=-1.0)
+
+        early_stages = [new_values_stage(), new_values_stage()]
+
+        def down_pair(j0):
+            tiles = [project_down(j) for j in (j0, j0 + 1)]
+            for c in range(2):
+                quantise_latent(j0 + c, tiles[c])
+
+        def early_values_pair(j0):
+            for j in (j0, j0 + 1):
+                for n in range(2):
+                    values(n, j, early_stages[n])
+
+        for j0 in range(0, CHUNKS, 2):
+            tiles = [flip(j) for j in (j0, j0 + 1)]
+            for c in range(2):
+                quantise_x(j0 + c, tiles[c])
+            if j0 >= 2:
+                down_pair(j0 - 2)
+            if j0 >= 4:
+                early_values_pair(j0 - 4)
+            if j0 == 0:
+                prepare_up(v_up_raw, v_up_codes, v_up_scales, 0)
+            else:
+                prepare_rope(j0 // 2 - 1)
+        down_pair(CHUNKS - 2)
+        early_values_pair(CHUNKS - 4)
+        early_values_pair(CHUNKS - 2)
+        for n in range(2):
+            store_values(n, early_stages[n])
+
+        prepare_rope(PASSES - 1)
+        prepare_up(v_up_raw, v_up_codes, v_up_scales, 1)
+        prepare_up(k_up_raw, k_up_codes, k_up_scales, 0)
+        prepare_up(k_up_raw, k_up_codes, k_up_scales, 1)
+
+        for n in range(2, GROUPS):
+            stage = new_values_stage()
+            for j in range(CHUNKS):
+                values(n, j, stage)
+            store_values(n, stage)
+
+        for n in range(GROUPS):
+            stage = stage_pool.tile([P, GROUP, CHUNKS, HEAD + ROT], F32, tag="stage", name="stage_k")
+            for j0 in range(0, CHUNKS, 2):
+                acc_r = rotary(n, j0)
+                for j in (j0, j0 + 1):
+                    project_up(k_up_codes, k_up_scales, n, j, stage[:, :, j, 0:HEAD])
+                rotate(acc_r, j0, stage)
+            nc.sync.dma_start(out=keys_view[:, GROUP * n : GROUP * n + GROUP, :, :], in_=stage[:])

@@ -29,6 +29,7 @@ PASSES = MODEL // K_PASS
 GROUP = BANK // HEAD
 GROUPS = HEADS // GROUP
 ROT_COLS = GROUP * ROT
+STORE_CHUNKS = 4
 
 FLOPS = 2 * TOKENS * (MODEL * LATENT + 2 * LATENT * HEADS * HEAD + MODEL * HEADS * ROT)
 
@@ -43,7 +44,7 @@ def tile_multiheadlatentattention_pb_kernel(
         raw_pool = ctx.enter_context(tc.tile_pool(name="raw", bufs=6))
         grouped_pool = ctx.enter_context(tc.tile_pool(name="grouped", bufs=4))
         rot_pool = ctx.enter_context(tc.tile_pool(name="rot", bufs=2))
-        stage_pool = ctx.enter_context(tc.tile_pool(name="stage", bufs=3))
+        stage_pool = ctx.enter_context(tc.tile_pool(name="stage", bufs=6))
         psum = ctx.enter_context(tc.psum_pool(name="psum", bufs=8))
         ctx.enter_context(tc.manual_schedule())
 
@@ -86,12 +87,14 @@ def tile_multiheadlatentattention_pb_kernel(
         down_raw = [load_down(0), load_down(1)]
         x_raw = [load_x(0)]
         v_up_raw = [load_up(W_v_up, 0)]
-        rope_raw = []
-        for c in range(1, CHUNKS // 2):
-            x_raw.append(load_x(c))
-            rope_raw.append(load_rope(c - 1))
-        rope_raw.append(load_rope(PASSES - 1))
+        x_raw.append(load_x(1))
+        rope_raw = [load_rope(0)]
+        x_raw.append(load_x(2))
+        rope_raw.append(load_rope(1))
+        x_raw.append(load_x(3))
         v_up_raw.append(load_up(W_v_up, 1))
+        rope_raw.append(load_rope(2))
+        rope_raw.append(load_rope(3))
         k_up_raw = [load_up(W_k_up, 0), load_up(W_k_up, 1)]
 
         ident = const.tile([P, P], F32)
@@ -208,14 +211,16 @@ def tile_multiheadlatentattention_pb_kernel(
         values_view = out_1.rearrange("b h (p j) d -> p (b h) j d", j=CHUNKS)
         keys_view = out_0.rearrange("b h (p j) d -> p (b h) j d", j=CHUNKS)
 
-        def new_values_stage():
-            return stage_pool.tile([P, GROUP, CHUNKS, HEAD], F32, tag="stage", name="stage_v")
+        def new_stage(features):
+            return stage_pool.tile([P, GROUP, STORE_CHUNKS, features], F32, tag="stage", name="stage")
+
+        def store(view, n, first_chunk, stage):
+            nc.sync.dma_start(
+                out=view[:, GROUP * n : GROUP * n + GROUP, first_chunk : first_chunk + STORE_CHUNKS, :], in_=stage[:]
+            )
 
         def values(n, j, stage):
-            project_up(v_up_codes, v_up_scales, n, j, stage[:, :, j, :])
-
-        def store_values(n, stage):
-            nc.sync.dma_start(out=values_view[:, GROUP * n : GROUP * n + GROUP, :, :], in_=stage[:])
+            project_up(v_up_codes, v_up_scales, n, j, stage[:, :, j % STORE_CHUNKS, :])
 
         def rotary(n, j0):
             rot_cols = slice(ROT_COLS * n, ROT_COLS * n + ROT_COLS)
@@ -235,6 +240,7 @@ def tile_multiheadlatentattention_pb_kernel(
 
         def rotate(acc_r, j0, stage):
             two = slice(j0, j0 + 2)
+            two_staged = slice(j0 % STORE_CHUNKS, j0 % STORE_CHUNKS + 2)
             by_feature = acc_r[:].rearrange("p (c h f) -> p c h f", c=2, h=GROUP)
             by_pair = acc_r[:].rearrange("p (c h i e) -> p c h i e", c=2, h=GROUP, e=2)
             with_cos = rot_pool.tile([P, 2, GROUP, PAIRS, 2], F32, tag="with_cos", name="with_cos")
@@ -258,7 +264,7 @@ def tile_multiheadlatentattention_pb_kernel(
                 op=MULT,
             )
             nc.gpsimd.tensor_tensor(
-                out=stage[:, :, two, HEAD : HEAD + ROT].rearrange("p h c (i e) -> p c h i e", e=2),
+                out=stage[:, :, two_staged, HEAD : HEAD + ROT].rearrange("p h c (i e) -> p c h i e", e=2),
                 in0=with_cos[:],
                 in1=with_sin[:].rearrange("p e c h i -> p c h i e"),
                 op=ADD,
@@ -276,7 +282,7 @@ def tile_multiheadlatentattention_pb_kernel(
         sin_minus = const.tile([P, CHUNKS, PAIRS], F32)
         nc.vector.tensor_scalar_mul(out=sin_minus[:], in0=sin_bf[:], scalar1=-1.0)
 
-        early_stages = [new_values_stage(), new_values_stage()]
+        early_stages = {}
 
         def down_pair(j0):
             tiles = [project_down(j) for j in (j0, j0 + 1)]
@@ -284,9 +290,15 @@ def tile_multiheadlatentattention_pb_kernel(
                 quantise_latent(j0 + c, tiles[c])
 
         def early_values_pair(j0):
+            for n in range(2):
+                if j0 % STORE_CHUNKS == 0:
+                    early_stages[n] = new_stage(HEAD)
             for j in (j0, j0 + 1):
                 for n in range(2):
                     values(n, j, early_stages[n])
+            for n in range(2):
+                if (j0 + 2) % STORE_CHUNKS == 0:
+                    store(values_view, n, j0 + 2 - STORE_CHUNKS, early_stages[n])
 
         for j0 in range(0, CHUNKS, 2):
             tiles = [flip(j) for j in (j0, j0 + 1)]
@@ -298,30 +310,32 @@ def tile_multiheadlatentattention_pb_kernel(
                 early_values_pair(j0 - 4)
             if j0 == 0:
                 prepare_up(v_up_raw, v_up_codes, v_up_scales, 0)
+            elif j0 == CHUNKS - 2:
+                prepare_up(v_up_raw, v_up_codes, v_up_scales, 1)
             else:
                 prepare_rope(j0 // 2 - 1)
         down_pair(CHUNKS - 2)
         early_values_pair(CHUNKS - 4)
         early_values_pair(CHUNKS - 2)
-        for n in range(2):
-            store_values(n, early_stages[n])
 
-        prepare_rope(PASSES - 1)
-        prepare_up(v_up_raw, v_up_codes, v_up_scales, 1)
+        prepare_rope(2)
+        prepare_rope(3)
         prepare_up(k_up_raw, k_up_codes, k_up_scales, 0)
         prepare_up(k_up_raw, k_up_codes, k_up_scales, 1)
 
         for n in range(2, GROUPS):
-            stage = new_values_stage()
-            for j in range(CHUNKS):
-                values(n, j, stage)
-            store_values(n, stage)
+            for first_chunk in range(0, CHUNKS, STORE_CHUNKS):
+                stage = new_stage(HEAD)
+                for j in range(first_chunk, first_chunk + STORE_CHUNKS):
+                    values(n, j, stage)
+                store(values_view, n, first_chunk, stage)
 
         for n in range(GROUPS):
-            stage = stage_pool.tile([P, GROUP, CHUNKS, HEAD + ROT], F32, tag="stage", name="stage_k")
-            for j0 in range(0, CHUNKS, 2):
-                acc_r = rotary(n, j0)
-                for j in (j0, j0 + 1):
-                    project_up(k_up_codes, k_up_scales, n, j, stage[:, :, j, 0:HEAD])
-                rotate(acc_r, j0, stage)
-            nc.sync.dma_start(out=keys_view[:, GROUP * n : GROUP * n + GROUP, :, :], in_=stage[:])
+            for first_chunk in range(0, CHUNKS, STORE_CHUNKS):
+                stage = new_stage(HEAD + ROT)
+                for j0 in range(first_chunk, first_chunk + STORE_CHUNKS, 2):
+                    acc_r = rotary(n, j0)
+                    for j in (j0, j0 + 1):
+                        project_up(k_up_codes, k_up_scales, n, j, stage[:, :, j % STORE_CHUNKS, 0:HEAD])
+                    rotate(acc_r, j0, stage)
+                store(keys_view, n, first_chunk, stage)

@@ -29,7 +29,7 @@ PASSES = MODEL // K_PASS
 GROUP = BANK // HEAD
 GROUPS = HEADS // GROUP
 ROT_COLS = GROUP * ROT
-STORE_CHUNKS = 4
+STORE_CHUNKS = 8
 
 FLOPS = 2 * TOKENS * (MODEL * LATENT + 2 * LATENT * HEADS * HEAD + MODEL * HEADS * ROT)
 
@@ -44,7 +44,7 @@ def tile_multiheadlatentattention_pb_kernel(
         raw_pool = ctx.enter_context(tc.tile_pool(name="raw", bufs=6))
         grouped_pool = ctx.enter_context(tc.tile_pool(name="grouped", bufs=4))
         rot_pool = ctx.enter_context(tc.tile_pool(name="rot", bufs=2))
-        stage_pool = ctx.enter_context(tc.tile_pool(name="stage", bufs=6))
+        stage_pool = ctx.enter_context(tc.tile_pool(name="stage", bufs=24 // STORE_CHUNKS))
         psum = ctx.enter_context(tc.psum_pool(name="psum", bufs=8))
         ctx.enter_context(tc.manual_schedule())
 
@@ -117,11 +117,25 @@ def tile_multiheadlatentattention_pb_kernel(
                 out=codes.bitcast(FP8X4), scales=scales, in_=grouped[:].rearrange("p n t -> p (n t)")
             )
 
-        def prepare(first, second, second_copy=nc.vector.tensor_copy):
-            grouped_first = regroup(nc.vector.tensor_copy, first[0])
-            grouped_second = regroup(second_copy, second[0])
-            quantise(grouped_first, first[1], first[2])
-            quantise(grouped_second, second[1], second[2])
+        def prepare_steps(halves, second_copy=nc.vector.tensor_copy):
+            grouped = {}
+
+            def copy_half(i, copy):
+                grouped[i] = regroup(copy, halves[i][0])
+
+            def quantise_half(i):
+                quantise(grouped[i], halves[i][1], halves[i][2])
+
+            return [
+                lambda: copy_half(0, nc.vector.tensor_copy),
+                lambda: copy_half(1, second_copy),
+                lambda: quantise_half(0),
+                lambda: quantise_half(1),
+            ]
+
+        def prepare(halves, second_copy=nc.vector.tensor_copy):
+            for step in prepare_steps(halves, second_copy):
+                step()
 
         def prepare_down(c):
             rows = down_raw[c][:].rearrange("p s (e n) -> p (s e) n", e=2)
@@ -129,7 +143,7 @@ def tile_multiheadlatentattention_pb_kernel(
                 (rows[:, PACK * i : PACK * i + PACK, :], down_codes[:, 2 * c + i, :], down_scales[:, 2 * c + i, :])
                 for i in range(2)
             ]
-            prepare(halves[0], halves[1], second_copy=nc.scalar.copy)
+            prepare(halves, second_copy=nc.scalar.copy)
 
         def prepare_rope(g):
             rows = rope_raw[g][:].rearrange("p s (e n) -> p (s e) n", e=2)
@@ -138,15 +152,14 @@ def tile_multiheadlatentattention_pb_kernel(
                  rope_scales[:, g, BANK * i : BANK * i + BANK])
                 for i in range(2)
             ]
-            prepare(halves[0], halves[1])
+            prepare(halves)
 
-        def prepare_up(raw, codes, scales, c):
-            halves = [
+        def up_halves(raw, codes, scales, c):
+            return [
                 (raw[c][:, :, BANK * i : BANK * i + BANK], codes[:, BANK * (2 * c + i) : BANK * (2 * c + i + 1)],
                  scales[:, BANK * (2 * c + i) : BANK * (2 * c + i + 1)])
                 for i in range(2)
             ]
-            prepare(halves[0], halves[1])
 
         def flip(j):
             words = x_raw[j // 2][:, j % 2, :].bitcast(F32)
@@ -289,16 +302,12 @@ def tile_multiheadlatentattention_pb_kernel(
             for c in range(2):
                 quantise_latent(j0 + c, tiles[c])
 
-        def early_values_pair(j0):
-            for n in range(2):
-                if j0 % STORE_CHUNKS == 0:
-                    early_stages[n] = new_stage(HEAD)
-            for j in (j0, j0 + 1):
-                for n in range(2):
-                    values(n, j, early_stages[n])
-            for n in range(2):
-                if (j0 + 2) % STORE_CHUNKS == 0:
-                    store(values_view, n, j0 + 2 - STORE_CHUNKS, early_stages[n])
+        def early_values(n, j):
+            if j % STORE_CHUNKS == 0:
+                early_stages[n] = new_stage(HEAD)
+            values(n, j, early_stages[n])
+            if (j + 1) % STORE_CHUNKS == 0:
+                store(values_view, n, j + 1 - STORE_CHUNKS, early_stages[n])
 
         for j0 in range(0, CHUNKS, 2):
             tiles = [flip(j) for j in (j0, j0 + 1)]
@@ -307,21 +316,24 @@ def tile_multiheadlatentattention_pb_kernel(
             if j0 >= 2:
                 down_pair(j0 - 2)
             if j0 >= 4:
-                early_values_pair(j0 - 4)
+                for j in (j0 - 4, j0 - 3):
+                    for n in range(2):
+                        early_values(n, j)
             if j0 == 0:
-                prepare_up(v_up_raw, v_up_codes, v_up_scales, 0)
+                prepare(up_halves(v_up_raw, v_up_codes, v_up_scales, 0))
             elif j0 == CHUNKS - 2:
-                prepare_up(v_up_raw, v_up_codes, v_up_scales, 1)
+                prepare(up_halves(v_up_raw, v_up_codes, v_up_scales, 1))
             else:
                 prepare_rope(j0 // 2 - 1)
         down_pair(CHUNKS - 2)
-        early_values_pair(CHUNKS - 4)
-        early_values_pair(CHUNKS - 2)
+        for n in range(2):
+            for j in range(CHUNKS - 4, CHUNKS):
+                early_values(n, j)
 
         prepare_rope(2)
         prepare_rope(3)
-        prepare_up(k_up_raw, k_up_codes, k_up_scales, 0)
-        prepare_up(k_up_raw, k_up_codes, k_up_scales, 1)
+        prepare(up_halves(k_up_raw, k_up_codes, k_up_scales, 0))
+        late_steps = prepare_steps(up_halves(k_up_raw, k_up_codes, k_up_scales, 1))
 
         for n in range(2, GROUPS):
             for first_chunk in range(0, CHUNKS, STORE_CHUNKS):
@@ -338,4 +350,6 @@ def tile_multiheadlatentattention_pb_kernel(
                     for j in (j0, j0 + 1):
                         project_up(k_up_codes, k_up_scales, n, j, stage[:, :, j % STORE_CHUNKS, 0:HEAD])
                     rotate(acc_r, j0, stage)
+                    if n == 0:
+                        late_steps[j0 // 2]()
                 store(keys_view, n, first_chunk, stage)

@@ -29,7 +29,7 @@ PASSES = MODEL // K_PASS
 GROUP = BANK // HEAD
 GROUPS = HEADS // GROUP
 ROT_COLS = GROUP * ROT
-STORE_CHUNKS = 8
+STORE_CHUNKS = 4
 
 FLOPS = 2 * TOKENS * (MODEL * LATENT + 2 * LATENT * HEADS * HEAD + MODEL * HEADS * ROT)
 

@@ -104,6 +104,12 @@ def tile_multiheadlatentattention_pb_kernel(
         nc.scalar.dma_start(out=cos_bf[:], in_=rope_cos.rearrange("(p j) i -> p j i", j=CHUNKS))
         nc.scalar.dma_start(out=sin_bf[:], in_=rope_sin.rearrange("(p j) i -> p j i", j=CHUNKS))
 
+        cos_twice = const.tile([P, CHUNKS, PAIRS, 2], F32)
+        sin_signed = const.tile([P, CHUNKS, PAIRS, 2], F32)
+        nc.gpsimd.tensor_copy(out=cos_twice[:], in_=cos_bf[:].unsqueeze(3).to_broadcast([P, CHUNKS, PAIRS, 2]))
+        nc.gpsimd.tensor_scalar(out=sin_signed[:, :, :, 0], in0=sin_bf[:], scalar1=-1.0, scalar2=0.0, op0=MULT, op1=ADD)
+        nc.gpsimd.tensor_copy(out=sin_signed[:, :, :, 1], in_=sin_bf[:])
+
         def regroup(copy, rows):
             grouped = grouped_pool.tile([P, BANK, PACK], BF16, tag="grouped", name="grouped", align_bytes=64)
             copy(
@@ -263,37 +269,22 @@ def tile_multiheadlatentattention_pb_kernel(
                 in1=cos_twice[:, two, :, :].rearrange("p c i e -> p c (i e)").unsqueeze(2).to_broadcast([P, 2, GROUP, ROT]),
                 op=MULT,
             )
-            with_sin = rot_pool.tile([P, 2, 2, GROUP, PAIRS], F32, tag="with_sin", name="with_sin")
+            with_sin = rot_pool.tile([P, 2, GROUP, PAIRS, 2], F32, tag="with_sin", name="with_sin")
             nc.vector.tensor_tensor(
-                out=with_sin[:, 0, :, :, :],
-                in0=by_pair[:, :, :, :, 1],
-                in1=sin_minus[:, two, :].unsqueeze(2).to_broadcast([P, 2, GROUP, PAIRS]),
-                op=MULT,
-            )
-            nc.vector.tensor_tensor(
-                out=with_sin[:, 1, :, :, :],
-                in0=by_pair[:, :, :, :, 0],
-                in1=sin_plus[:, two, :].unsqueeze(2).to_broadcast([P, 2, GROUP, PAIRS]),
+                out=with_sin[:],
+                in0=by_pair[:, :, :, :, ::-1],
+                in1=sin_signed[:, two, :, :].unsqueeze(2).to_broadcast([P, 2, GROUP, PAIRS, 2]),
                 op=MULT,
             )
             nc.gpsimd.tensor_tensor(
                 out=stage[:, :, two_staged, HEAD : HEAD + ROT].rearrange("p h c (i e) -> p c h i e", e=2),
                 in0=with_cos[:],
-                in1=with_sin[:].rearrange("p e c h i -> p c h i e"),
+                in1=with_sin[:],
                 op=ADD,
             )
 
         prepare_down(0)
         prepare_down(1)
-
-        cos_twice = const.tile([P, CHUNKS, PAIRS, 2], F32)
-        nc.vector.tensor_copy(
-            out=cos_twice[:], in_=cos_bf[:].unsqueeze(3).to_broadcast([P, CHUNKS, PAIRS, 2])
-        )
-        sin_plus = const.tile([P, CHUNKS, PAIRS], F32)
-        nc.vector.tensor_copy(out=sin_plus[:], in_=sin_bf[:])
-        sin_minus = const.tile([P, CHUNKS, PAIRS], F32)
-        nc.vector.tensor_scalar_mul(out=sin_minus[:], in0=sin_bf[:], scalar1=-1.0)
 
         early_stages = {}
 

@@ -151,14 +151,13 @@ def tile_multiheadlatentattention_pb_kernel(
             ]
             prepare(halves, second_copy=nc.scalar.copy)
 
-        def prepare_rope(g):
+        def rope_part(g, h):
             rows = rope_raw[g][:].rearrange("p s (e n) -> p (s e) n", e=2)
-            halves = [
-                (rows[:, :, BANK * i : BANK * i + BANK], rope_codes[:, g, BANK * i : BANK * i + BANK],
-                 rope_scales[:, g, BANK * i : BANK * i + BANK])
-                for i in range(2)
-            ]
-            prepare(halves)
+            cols = slice(BANK * h, BANK * h + BANK)
+            return rows[:, :, cols], rope_codes[:, g, cols], rope_scales[:, g, cols]
+
+        def prepare_rope(g):
+            prepare([rope_part(g, h) for h in range(2)])
 
         def up_halves(raw, codes, scales, c):
             return [
@@ -233,8 +232,8 @@ def tile_multiheadlatentattention_pb_kernel(
         def new_stage(features):
             return stage_pool.tile([P, GROUP, STORE_CHUNKS, features], F32, tag="stage", name="stage")
 
-        def store(view, n, first_chunk, stage):
-            nc.sync.dma_start(
+        def store(view, n, first_chunk, stage, queue=nc.sync):
+            queue.dma_start(
                 out=view[:, GROUP * n : GROUP * n + GROUP, first_chunk : first_chunk + STORE_CHUNKS, :], in_=stage[:]
             )
 
@@ -288,8 +287,10 @@ def tile_multiheadlatentattention_pb_kernel(
 
         early_stages = {}
 
-        def down_pair(j0):
-            tiles = [project_down(j) for j in (j0, j0 + 1)]
+        def project_pair(j0):
+            return [project_down(j) for j in (j0, j0 + 1)]
+
+        def quantise_pair(j0, tiles):
             for c in range(2):
                 quantise_latent(j0 + c, tiles[c])
 
@@ -300,23 +301,32 @@ def tile_multiheadlatentattention_pb_kernel(
             if (j + 1) % STORE_CHUNKS == 0:
                 store(values_view, n, j + 1 - STORE_CHUNKS, early_stages[n])
 
+        rope_steps = [prepare_steps([rope_part(g, h) for h in range(2)]) for g in range(2)]
+        fillers = [
+            prepare_steps(up_halves(v_up_raw, v_up_codes, v_up_scales, 0), second_copy=nc.scalar.copy),
+            rope_steps[0],
+            rope_steps[1],
+            prepare_steps(up_halves(v_up_raw, v_up_codes, v_up_scales, 1)),
+        ]
         for j0 in range(0, CHUNKS, 2):
             tiles = [flip(j) for j in (j0, j0 + 1)]
             for c in range(2):
                 quantise_x(j0 + c, tiles[c])
+            steps = fillers[j0 // 2]
             if j0 >= 2:
-                down_pair(j0 - 2)
+                latents = project_pair(j0 - 2)
+            for step in steps[:2]:
+                step()
+            if j0 >= 2:
+                quantise_pair(j0 - 2, latents)
+            for step in steps[2:]:
+                step()
             if j0 >= 4:
                 for j in (j0 - 4, j0 - 3):
                     for n in range(2):
                         early_values(n, j)
-            if j0 == 0:
-                prepare(up_halves(v_up_raw, v_up_codes, v_up_scales, 0))
-            elif j0 == CHUNKS - 2:
-                prepare(up_halves(v_up_raw, v_up_codes, v_up_scales, 1))
-            else:
-                prepare_rope(j0 // 2 - 1)
-        down_pair(CHUNKS - 2)
+        latents = project_pair(CHUNKS - 2)
+        quantise_pair(CHUNKS - 2, latents)
         for n in range(2):
             for j in range(CHUNKS - 4, CHUNKS):
                 early_values(n, j)
@@ -326,21 +336,33 @@ def tile_multiheadlatentattention_pb_kernel(
         prepare(up_halves(k_up_raw, k_up_codes, k_up_scales, 0))
         late_steps = prepare_steps(up_halves(k_up_raw, k_up_codes, k_up_scales, 1))
 
+        units = [(n, first_chunk) for n in range(GROUPS) for first_chunk in range(0, CHUNKS, STORE_CHUNKS)]
+        rotary_steps = [(u, j0) for u in range(len(units)) for j0 in range(0, STORE_CHUNKS, 2)]
+        stages = {}
+
+        def next_rotary():
+            u, j0 = rotary_steps.pop(0)
+            n, first_chunk = units[u]
+            if j0 == 0:
+                stages[u] = new_stage(HEAD + ROT)
+            rotate(rotary(n, first_chunk + j0), first_chunk + j0, stages[u])
+
         for n in range(2, GROUPS):
             for first_chunk in range(0, CHUNKS, STORE_CHUNKS):
                 stage = new_stage(HEAD)
                 for j in range(first_chunk, first_chunk + STORE_CHUNKS):
                     values(n, j, stage)
+                    if n == GROUPS - 1 and j in (1, 3, 5):
+                        next_rotary()
                 store(values_view, n, first_chunk, stage)
 
-        for n in range(GROUPS):
-            for first_chunk in range(0, CHUNKS, STORE_CHUNKS):
-                stage = new_stage(HEAD + ROT)
-                for j0 in range(first_chunk, first_chunk + STORE_CHUNKS, 2):
-                    acc_r = rotary(n, j0)
-                    for j in (j0, j0 + 1):
-                        project_up(k_up_codes, k_up_scales, n, j, stage[:, :, j % STORE_CHUNKS, 0:HEAD])
-                    rotate(acc_r, j0, stage)
-                    if n == 0:
-                        late_steps[j0 // 2]()
-                store(keys_view, n, first_chunk, stage)
+
+        for u, (n, first_chunk) in enumerate(units):
+            for j in range(first_chunk, first_chunk + STORE_CHUNKS):
+                project_up(k_up_codes, k_up_scales, n, j, stages[u][:, :, j % STORE_CHUNKS, 0:HEAD])
+                if j % 2 == 1:
+                    if rotary_steps:
+                        next_rotary()
+                    if late_steps:
+                        late_steps.pop(0)()
+            store(keys_view, n, first_chunk, stages[u])

@@ -28,6 +28,7 @@ CHUNKS = TOKENS // P
 PASSES = MODEL // K_PASS
 GROUP = BANK // HEAD
 GROUPS = HEADS // GROUP
+PAIR = 2
 ROT_COLS = GROUP * ROT
 STORE_CHUNKS = 4
 
@@ -229,6 +230,27 @@ def tile_multiheadlatentattention_pb_kernel(
         values_view = out_1.rearrange("b h (p j) d -> p (b h) j d", j=CHUNKS)
         keys_view = out_0.rearrange("b h (p j) d -> p (b h) j d", j=CHUNKS)
 
+        def values_of_pair(q, behind_bank):
+            stage = stage_pool.tile([P, PAIR, CHUNKS, HEAD], F32, tag="stage", name="stage")
+            cols = slice(PAIR * HEAD * q, PAIR * HEAD * q + PAIR * HEAD)
+            for j0 in range(0, CHUNKS, 2):
+                acc = psum.tile([P, BANK], F32, tag="bank", name="acc")
+                for c in range(2):
+                    nc.tensor.matmul_mx(
+                        out=acc[:, PAIR * HEAD * c : PAIR * HEAD * c + PAIR * HEAD],
+                        lhsT=latent_codes[:, j0 + c, :].bitcast(FP8X4),
+                        lhsT_scale=latent_scales[:, j0 + c, :],
+                        rhs=v_up_codes[:, cols].bitcast(FP8X4),
+                        rhs_scale=v_up_scales[:, cols],
+                        start=True,
+                        stop=True,
+                    )
+                nc.scalar.copy(
+                    out=stage[:, :, j0 : j0 + 2, :], in_=acc[:].rearrange("p (c h d) -> p h c d", c=2, h=PAIR)
+                )
+                behind_bank(q, j0)
+            nc.sync.dma_start(out=values_view[:, PAIR * q : PAIR * q + PAIR, :, :], in_=stage[:])
+
         def new_stage(features):
             return stage_pool.tile([P, GROUP, STORE_CHUNKS, features], F32, tag="stage", name="stage")
 
@@ -347,15 +369,12 @@ def tile_multiheadlatentattention_pb_kernel(
                 stages[u] = new_stage(HEAD + ROT)
             rotate(rotary(n, first_chunk + j0), first_chunk + j0, stages[u])
 
-        for n in range(2, GROUPS):
-            for first_chunk in range(0, CHUNKS, STORE_CHUNKS):
-                stage = new_stage(HEAD)
-                for j in range(first_chunk, first_chunk + STORE_CHUNKS):
-                    values(n, j, stage)
-                    if n == GROUPS - 1 and j in (1, 3, 5):
-                        next_rotary()
-                store(values_view, n, first_chunk, stage)
+        def behind_bank(q, j0):
+            if (q, j0) in ((6, 2), (6, 6), (7, 2)):
+                next_rotary()
 
+        for q in range(4, HEADS // PAIR):
+            values_of_pair(q, behind_bank)
 
         for u, (n, first_chunk) in enumerate(units):
             for j in range(first_chunk, first_chunk + STORE_CHUNKS):

@@ -42,7 +42,8 @@ def tile_multiheadlatentattention_pb_kernel(
     with ExitStack() as ctx:
         const = ctx.enter_context(tc.tile_pool(name="const", bufs=1))
         keep = ctx.enter_context(tc.tile_pool(name="keep", bufs=1))
-        raw_pool = ctx.enter_context(tc.tile_pool(name="raw", bufs=6))
+        raw_pool = ctx.enter_context(tc.tile_pool(name="raw", bufs=5))
+        whole_pool = ctx.enter_context(tc.tile_pool(name="whole", bufs=1))
         grouped_pool = ctx.enter_context(tc.tile_pool(name="grouped", bufs=4))
         rot_pool = ctx.enter_context(tc.tile_pool(name="rot", bufs=2))
         stage_pool = ctx.enter_context(tc.tile_pool(name="stage", bufs=24 // STORE_CHUNKS))
@@ -85,6 +86,13 @@ def tile_multiheadlatentattention_pb_kernel(
             view = weight.rearrange("(t p) n -> p t n", p=P)
             return load([P, PACK, 2 * BANK], view[:, :, 2 * BANK * c : 2 * BANK * (c + 1)])
 
+        def load_up_whole(weight):
+            view = weight.rearrange("(t p) n -> p t n", p=P)
+            raw = whole_pool.tile([P, PACK, HEADS * HEAD], BF16, tag="whole", name="whole")
+            for t in (0, 2):
+                nc.sync.dma_start(out=raw[:, t : t + 2, :], in_=view[:, t : t + 2, :])
+            return [raw[:, :, 2 * BANK * c : 2 * BANK * (c + 1)] for c in range(2)]
+
         down_raw = [load_down(0), load_down(1)]
         x_raw = [load_x(0)]
         v_up_raw = [load_up(W_v_up, 0)]
@@ -96,7 +104,7 @@ def tile_multiheadlatentattention_pb_kernel(
         v_up_raw.append(load_up(W_v_up, 1))
         rope_raw.append(load_rope(2))
         rope_raw.append(load_rope(3))
-        k_up_raw = [load_up(W_k_up, 0), load_up(W_k_up, 1)]
+        k_up_raw = load_up_whole(W_k_up)
 
         ident = const.tile([P, P], F32)
         make_identity(nc, ident[:])
@@ -335,18 +343,18 @@ def tile_multiheadlatentattention_pb_kernel(
             for c in range(2):
                 quantise_x(j0 + c, tiles[c])
             steps = fillers[j0 // 2]
+            between = 0 if j0 == 4 else 2
             if j0 >= 2:
                 latents = project_pair(j0 - 2)
-            for step in steps[:2]:
+            for step in steps[:between]:
                 step()
             if j0 >= 2:
                 quantise_pair(j0 - 2, latents)
-            for step in steps[2:]:
+            for step in steps[between:]:
                 step()
             if j0 >= 4:
-                for j in (j0 - 4, j0 - 3):
-                    for n in range(2):
-                        early_values(n, j)
+                for j in range(STORE_CHUNKS):
+                    early_values(j0 // 2 - 2, j)
         latents = project_pair(CHUNKS - 2)
         quantise_pair(CHUNKS - 2, latents)
         for n in range(2):
@@ -379,9 +387,8 @@ def tile_multiheadlatentattention_pb_kernel(
         for u, (n, first_chunk) in enumerate(units):
             for j in range(first_chunk, first_chunk + STORE_CHUNKS):
                 project_up(k_up_codes, k_up_scales, n, j, stages[u][:, :, j % STORE_CHUNKS, 0:HEAD])
-                if j % 2 == 1:
-                    if rotary_steps:
-                        next_rotary()
-                    if late_steps:
-                        late_steps.pop(0)()
+                if j % 2 == 1 and rotary_steps:
+                    next_rotary()
+                if j % STORE_CHUNKS == STORE_CHUNKS - 1 and late_steps:
+                    late_steps.pop(0)()
             store(keys_view, n, first_chunk, stages[u])

@@ -29,7 +29,9 @@ PASSES = MODEL // K_PASS
 GROUP = BANK // HEAD
 GROUPS = HEADS // GROUP
 PAIR = 2
-ROT_COLS = GROUP * ROT
+PAIRS_OF_HEADS = HEADS // PAIR
+ROT_COLS = PAIR * ROT
+ROT_CHUNKS = BANK // ROT_COLS
 STORE_CHUNKS = 4
 
 FLOPS = 2 * TOKENS * (MODEL * LATENT + 2 * LATENT * HEADS * HEAD + MODEL * HEADS * ROT)
@@ -238,26 +240,28 @@ def tile_multiheadlatentattention_pb_kernel(
         values_view = out_1.rearrange("b h (p j) d -> p (b h) j d", j=CHUNKS)
         keys_view = out_0.rearrange("b h (p j) d -> p (b h) j d", j=CHUNKS)
 
-        def values_of_pair(q, behind_bank):
-            stage = stage_pool.tile([P, PAIR, CHUNKS, HEAD], F32, tag="stage", name="stage")
+        def project_pair_up(codes, scales, q, j0, stage):
             cols = slice(PAIR * HEAD * q, PAIR * HEAD * q + PAIR * HEAD)
-            for j0 in range(0, CHUNKS, 2):
-                acc = psum.tile([P, BANK], F32, tag="bank", name="acc")
-                for c in range(2):
-                    nc.tensor.matmul_mx(
-                        out=acc[:, PAIR * HEAD * c : PAIR * HEAD * c + PAIR * HEAD],
-                        lhsT=latent_codes[:, j0 + c, :].bitcast(FP8X4),
-                        lhsT_scale=latent_scales[:, j0 + c, :],
-                        rhs=v_up_codes[:, cols].bitcast(FP8X4),
-                        rhs_scale=v_up_scales[:, cols],
-                        start=True,
-                        stop=True,
-                    )
-                nc.scalar.copy(
-                    out=stage[:, :, j0 : j0 + 2, :], in_=acc[:].rearrange("p (c h d) -> p h c d", c=2, h=PAIR)
+            acc = psum.tile([P, BANK], F32, tag="bank", name="acc")
+            for c in range(2):
+                nc.tensor.matmul_mx(
+                    out=acc[:, PAIR * HEAD * c : PAIR * HEAD * c + PAIR * HEAD],
+                    lhsT=latent_codes[:, j0 + c, :].bitcast(FP8X4),
+                    lhsT_scale=latent_scales[:, j0 + c, :],
+                    rhs=codes[:, cols].bitcast(FP8X4),
+                    rhs_scale=scales[:, cols],
+                    start=True,
+                    stop=True,
                 )
-                behind_bank(q, j0)
-            nc.sync.dma_start(out=values_view[:, PAIR * q : PAIR * q + PAIR, :, :], in_=stage[:])
+            nc.scalar.copy(
+                out=stage[:, :, j0 : j0 + 2, 0:HEAD], in_=acc[:].rearrange("p (c h d) -> p h c d", c=2, h=PAIR)
+            )
+
+        def new_pair_stage(features):
+            return stage_pool.tile([P, PAIR, CHUNKS, features], F32, tag="stage", name="stage")
+
+        def store_pair(view, q, stage):
+            nc.sync.dma_start(out=view[:, PAIR * q : PAIR * q + PAIR, :, :], in_=stage[:])
 
         def new_stage(features):
             return stage_pool.tile([P, GROUP, STORE_CHUNKS, features], F32, tag="stage", name="stage")
@@ -270,10 +274,10 @@ def tile_multiheadlatentattention_pb_kernel(
         def values(n, j, stage):
             project_up(v_up_codes, v_up_scales, n, j, stage[:, :, j % STORE_CHUNKS, :])
 
-        def rotary(n, j0):
-            rot_cols = slice(ROT_COLS * n, ROT_COLS * n + ROT_COLS)
+        def rotary(q, j0):
+            rot_cols = slice(ROT_COLS * q, ROT_COLS * q + ROT_COLS)
             acc_r = psum.tile([P, BANK], F32, tag="bank", name="acc_r")
-            for c in range(2):
+            for c in range(ROT_CHUNKS):
                 for g in range(PASSES):
                     nc.tensor.matmul_mx(
                         out=acc_r[:, ROT_COLS * c : ROT_COLS * c + ROT_COLS],
@@ -287,26 +291,25 @@ def tile_multiheadlatentattention_pb_kernel(
             return acc_r
 
         def rotate(acc_r, j0, stage):
-            two = slice(j0, j0 + 2)
-            two_staged = slice(j0 % STORE_CHUNKS, j0 % STORE_CHUNKS + 2)
-            by_feature = acc_r[:].rearrange("p (c h f) -> p c h f", c=2, h=GROUP)
-            by_pair = acc_r[:].rearrange("p (c h i e) -> p c h i e", c=2, h=GROUP, e=2)
-            with_cos = rot_pool.tile([P, 2, GROUP, PAIRS, 2], F32, tag="with_cos", name="with_cos")
+            chunks = slice(j0, j0 + ROT_CHUNKS)
+            by_feature = acc_r[:].rearrange("p (c h f) -> p c h f", c=ROT_CHUNKS, h=PAIR)
+            by_pair = acc_r[:].rearrange("p (c h i e) -> p c h i e", c=ROT_CHUNKS, h=PAIR, e=2)
+            with_cos = rot_pool.tile([P, ROT_CHUNKS, PAIR, PAIRS, 2], F32, tag="with_cos", name="with_cos")
             nc.vector.tensor_tensor(
                 out=with_cos[:].rearrange("p c h i e -> p c h (i e)"),
                 in0=by_feature,
-                in1=cos_twice[:, two, :, :].rearrange("p c i e -> p c (i e)").unsqueeze(2).to_broadcast([P, 2, GROUP, ROT]),
+                in1=cos_twice[:, chunks, :, :].rearrange("p c i e -> p c (i e)").unsqueeze(2).to_broadcast([P, ROT_CHUNKS, PAIR, ROT]),
                 op=MULT,
             )
-            with_sin = rot_pool.tile([P, 2, GROUP, PAIRS, 2], F32, tag="with_sin", name="with_sin")
+            with_sin = rot_pool.tile([P, ROT_CHUNKS, PAIR, PAIRS, 2], F32, tag="with_sin", name="with_sin")
             nc.vector.tensor_tensor(
                 out=with_sin[:],
                 in0=by_pair[:, :, :, :, ::-1],
-                in1=sin_signed[:, two, :, :].unsqueeze(2).to_broadcast([P, 2, GROUP, PAIRS, 2]),
+                in1=sin_signed[:, chunks, :, :].unsqueeze(2).to_broadcast([P, ROT_CHUNKS, PAIR, PAIRS, 2]),
                 op=MULT,
             )
             nc.gpsimd.tensor_tensor(
-                out=stage[:, :, two_staged, HEAD : HEAD + ROT].rearrange("p h c (i e) -> p c h i e", e=2),
+                out=stage[:, :, chunks, HEAD : HEAD + ROT].rearrange("p h c (i e) -> p c h i e", e=2),
                 in0=with_cos[:],
                 in1=with_sin[:],
                 op=ADD,
@@ -366,29 +369,28 @@ def tile_multiheadlatentattention_pb_kernel(
         prepare(up_halves(k_up_raw, k_up_codes, k_up_scales, 0))
         late_steps = prepare_steps(up_halves(k_up_raw, k_up_codes, k_up_scales, 1))
 
-        units = [(n, first_chunk) for n in range(GROUPS) for first_chunk in range(0, CHUNKS, STORE_CHUNKS)]
-        rotary_steps = [(u, j0) for u in range(len(units)) for j0 in range(0, STORE_CHUNKS, 2)]
-        stages = {}
+        rotary_steps = [(q, j0) for q in range(PAIRS_OF_HEADS) for j0 in range(0, CHUNKS, ROT_CHUNKS)]
+        key_stages = {}
 
         def next_rotary():
-            u, j0 = rotary_steps.pop(0)
-            n, first_chunk = units[u]
+            q, j0 = rotary_steps.pop(0)
             if j0 == 0:
-                stages[u] = new_stage(HEAD + ROT)
-            rotate(rotary(n, first_chunk + j0), first_chunk + j0, stages[u])
+                key_stages[q] = new_pair_stage(HEAD + ROT)
+            rotate(rotary(q, j0), j0, key_stages[q])
 
-        def behind_bank(q, j0):
-            if (q, j0) in ((6, 2), (6, 6), (7, 2)):
-                next_rotary()
-
-        for q in range(4, HEADS // PAIR):
-            values_of_pair(q, behind_bank)
-
-        for u, (n, first_chunk) in enumerate(units):
-            for j in range(first_chunk, first_chunk + STORE_CHUNKS):
-                project_up(k_up_codes, k_up_scales, n, j, stages[u][:, :, j % STORE_CHUNKS, 0:HEAD])
-                if j % 2 == 1 and rotary_steps:
+        for q in range(PAIRS_OF_HEADS // 2, PAIRS_OF_HEADS):
+            stage = new_pair_stage(HEAD)
+            for j0 in range(0, CHUNKS, 2):
+                project_pair_up(v_up_codes, v_up_scales, q, j0, stage)
+                if q == PAIRS_OF_HEADS - 1 and j0 % 4 == 2:
                     next_rotary()
-                if j % STORE_CHUNKS == STORE_CHUNKS - 1 and late_steps:
-                    late_steps.pop(0)()
-            store(keys_view, n, first_chunk, stages[u])
+            store_pair(values_view, q, stage)
+
+        for q in range(PAIRS_OF_HEADS):
+            for j0 in range(0, CHUNKS, 2):
+                project_pair_up(k_up_codes, k_up_scales, q, j0, key_stages[q])
+                if j0 % 4 == 2 and rotary_steps:
+                    next_rotary()
+            if late_steps:
+                late_steps.pop(0)()
+            store_pair(keys_view, q, key_stages[q])

@@ -382,7 +382,7 @@ def tile_multiheadlatentattention_pb_kernel(
             stage = new_pair_stage(HEAD)
             for j0 in range(0, CHUNKS, 2):
                 project_pair_up(v_up_codes, v_up_scales, q, j0, stage)
-                if q == PAIRS_OF_HEADS - 1 and j0 % 4 == 2:
+                if (q, j0) in ((PAIRS_OF_HEADS - 2, CHUNKS - 2), (PAIRS_OF_HEADS - 1, CHUNKS // 2 - 2)):
                     next_rotary()
             store_pair(values_view, q, stage)
 

from contextlib import ExitStack

import concourse.mybir as mybir
from concourse.masks import make_identity

F32 = mybir.dt.float32
BF16 = mybir.dt.bfloat16
U32 = mybir.dt.uint32
U8 = mybir.dt.uint8
FP8X4 = mybir.dt.float8_e4m3fn_x4
MULT = mybir.AluOpType.mult
ADD = mybir.AluOpType.add

P = 128
PACK = 4
K_PASS = P * PACK
BANK = 512

TOKENS = 1024
MODEL = 2048
LATENT = 512
HEADS = 16
HEAD = 128
ROT = 64
PAIRS = ROT // 2

CHUNKS = TOKENS // P
PASSES = MODEL // K_PASS
GROUP = BANK // HEAD
GROUPS = HEADS // GROUP
PAIR = 2
PAIRS_OF_HEADS = HEADS // PAIR
ROT_COLS = PAIR * ROT
ROT_CHUNKS = BANK // ROT_COLS
STORE_CHUNKS = 4

FLOPS = 2 * TOKENS * (MODEL * LATENT + 2 * LATENT * HEADS * HEAD + MODEL * HEADS * ROT)


def tile_multiheadlatentattention_pb_kernel(
    tc, x, W_kv_down, W_k_up, W_v_up, W_k_rope, rope_cos, rope_sin, out_0, out_1
):
    nc = tc.nc
    with ExitStack() as ctx:
        const = ctx.enter_context(tc.tile_pool(name="const", bufs=1))
        keep = ctx.enter_context(tc.tile_pool(name="keep", bufs=1))
        raw_pool = ctx.enter_context(tc.tile_pool(name="raw", bufs=5))
        whole_pool = ctx.enter_context(tc.tile_pool(name="whole", bufs=1))
        grouped_pool = ctx.enter_context(tc.tile_pool(name="grouped", bufs=4))
        rot_pool = ctx.enter_context(tc.tile_pool(name="rot", bufs=2))
        stage_pool = ctx.enter_context(tc.tile_pool(name="stage", bufs=24 // STORE_CHUNKS))
        psum = ctx.enter_context(tc.psum_pool(name="psum", bufs=8))
        ctx.enter_context(tc.manual_schedule())

        x_codes = keep.tile([P, CHUNKS, PASSES, P], U32, align_bytes=64)
        x_scales = keep.tile([P, CHUNKS, PASSES, P], U8, align_bytes=64)
        down_codes = keep.tile([P, PASSES, LATENT], U32, align_bytes=64)
        down_scales = keep.tile([P, PASSES, LATENT], U8, align_bytes=64)
        rope_codes = keep.tile([P, PASSES, HEADS * ROT], U32, align_bytes=64)
        rope_scales = keep.tile([P, PASSES, HEADS * ROT], U8, align_bytes=64)
        latent_codes = keep.tile([P, CHUNKS, P], U32, align_bytes=64)
        latent_scales = keep.tile([P, CHUNKS, P], U8, align_bytes=64)
        k_up_codes = keep.tile([P, HEADS * HEAD], U32, align_bytes=64)
        k_up_scales = keep.tile([P, HEADS * HEAD], U8, align_bytes=64)
        v_up_codes = keep.tile([P, HEADS * HEAD], U32, align_bytes=64)
        v_up_scales = keep.tile([P, HEADS * HEAD], U8, align_bytes=64)

        def load(shape, source):
            raw = raw_pool.tile(shape, BF16, tag="raw", name="raw")
            nc.sync.dma_start(out=raw[:], in_=source)
            return raw

        x_view = x.rearrange("b (p j) k -> p (b j) k", j=CHUNKS)

        def load_x(c):
            return load([P, 2, MODEL], x_view[:, 2 * c : 2 * c + 2, :])

        down_view = W_kv_down.rearrange("(s q e) n -> q s (e n)", q=P, e=2)
        rope_view = W_k_rope.rearrange("(s q e) n -> q s (e n)", q=P, e=2)

        def load_down(c):
            return load([P, 4, 2 * LATENT], down_view[:, 4 * c : 4 * c + 4, :])

        def load_rope(g):
            return load([P, 2, 2 * HEADS * ROT], rope_view[:, 2 * g : 2 * g + 2, :])

        def load_up(weight, c):
            view = weight.rearrange("(t p) n -> p t n", p=P)
            return load([P, PACK, 2 * BANK], view[:, :, 2 * BANK * c : 2 * BANK * (c + 1)])

        def load_up_whole(weight):
            view = weight.rearrange("(t p) n -> p t n", p=P)
            raw = whole_pool.tile([P, PACK, HEADS * HEAD], BF16, tag="whole", name="whole")
            for t in (0, 2):
                nc.sync.dma_start(out=raw[:, t : t + 2, :], in_=view[:, t : t + 2, :])
            return [raw[:, :, 2 * BANK * c : 2 * BANK * (c + 1)] for c in range(2)]

        down_raw = [load_down(0), load_down(1)]
        x_raw = [load_x(0)]
        v_up_raw = [load_up(W_v_up, 0)]
        x_raw.append(load_x(1))
        rope_raw = [load_rope(0)]
        x_raw.append(load_x(2))
        rope_raw.append(load_rope(1))
        x_raw.append(load_x(3))
        v_up_raw.append(load_up(W_v_up, 1))
        rope_raw.append(load_rope(2))
        rope_raw.append(load_rope(3))
        k_up_raw = load_up_whole(W_k_up)

        ident = const.tile([P, P], F32)
        make_identity(nc, ident[:])
        cos_bf = const.tile([P, CHUNKS, PAIRS], BF16)
        sin_bf = const.tile([P, CHUNKS, PAIRS], BF16)
        nc.scalar.dma_start(out=cos_bf[:], in_=rope_cos.rearrange("(p j) i -> p j i", j=CHUNKS))
        nc.scalar.dma_start(out=sin_bf[:], in_=rope_sin.rearrange("(p j) i -> p j i", j=CHUNKS))

        cos_twice = const.tile([P, CHUNKS, PAIRS, 2], F32)
        sin_signed = const.tile([P, CHUNKS, PAIRS, 2], F32)
        nc.gpsimd.tensor_copy(out=cos_twice[:], in_=cos_bf[:].unsqueeze(3).to_broadcast([P, CHUNKS, PAIRS, 2]))
        nc.gpsimd.tensor_scalar(out=sin_signed[:, :, :, 0], in0=sin_bf[:], scalar1=-1.0, scalar2=0.0, op0=MULT, op1=ADD)
        nc.gpsimd.tensor_copy(out=sin_signed[:, :, :, 1], in_=sin_bf[:])

        def regroup(copy, rows):
            grouped = grouped_pool.tile([P, BANK, PACK], BF16, tag="grouped", name="grouped", align_bytes=64)
            copy(
                out=grouped[:].rearrange("p (c i) t -> p c t i", i=4),
                in_=rows.rearrange("p t (c i) -> p c t i", i=4),
            )
            return grouped

        def quantise(grouped, codes, scales):
            nc.vector.quantize_mx(
                out=codes.bitcast(FP8X4), scales=scales, in_=grouped[:].rearrange("p n t -> p (n t)")
            )

        def prepare_steps(halves, second_copy=nc.vector.tensor_copy):
            grouped = {}

            def copy_half(i, copy):
                grouped[i] = regroup(copy, halves[i][0])

            def quantise_half(i):
                quantise(grouped[i], halves[i][1], halves[i][2])

            return [
                lambda: copy_half(0, nc.vector.tensor_copy),
                lambda: copy_half(1, second_copy),
                lambda: quantise_half(0),
                lambda: quantise_half(1),
            ]

        def prepare(halves, second_copy=nc.vector.tensor_copy):
            for step in prepare_steps(halves, second_copy):
                step()

        def prepare_down(c):
            rows = down_raw[c][:].rearrange("p s (e n) -> p (s e) n", e=2)
            halves = [
                (rows[:, PACK * i : PACK * i + PACK, :], down_codes[:, 2 * c + i, :], down_scales[:, 2 * c + i, :])
                for i in range(2)
            ]
            prepare(halves, second_copy=nc.scalar.copy)

        def rope_part(g, h):
            rows = rope_raw[g][:].rearrange("p s (e n) -> p (s e) n", e=2)
            cols = slice(BANK * h, BANK * h + BANK)
            return rows[:, :, cols], rope_codes[:, g, cols], rope_scales[:, g, cols]

        def prepare_rope(g):
            prepare([rope_part(g, h) for h in range(2)])

        def up_halves(raw, codes, scales, c):
            return [
                (raw[c][:, :, BANK * i : BANK * i + BANK], codes[:, BANK * (2 * c + i) : BANK * (2 * c + i + 1)],
                 scales[:, BANK * (2 * c + i) : BANK * (2 * c + i + 1)])
                for i in range(2)
            ]

        def flip(j):
            words = x_raw[j // 2][:, j % 2, :].bitcast(F32)
            x_grouped = grouped_pool.tile([P, PASSES * P * PACK], BF16, tag="grouped", name="x_grouped", align_bytes=64)
            x_grouped_words = x_grouped[:].bitcast(F32).rearrange("p (g r u) -> p g r u", g=PASSES, u=2)
            for b in range(2):
                flipped = psum.tile([P, BANK], F32, tag="bank", name="flipped")
                for w in range(4):
                    first = P * (4 * b + w)
                    nc.tensor.transpose(flipped[:, P * w : P * w + P], words[:, first : first + P], ident[:])
                nc.scalar.copy(
                    out=x_grouped_words[:, 2 * b : 2 * b + 2, :, :],
                    in_=flipped[:].rearrange("p (g u r) -> p g r u", g=2, u=2),
                )
            return x_grouped

        def quantise_x(j, x_grouped):
            nc.vector.quantize_mx(
                out=x_codes[:, j, :, :].rearrange("p g r -> p (g r)").bitcast(FP8X4),
                scales=x_scales[:, j, :, :].rearrange("p g r -> p (g r)"),
                in_=x_grouped[:],
            )

        def project_down(j):
            latent = psum.tile([P, BANK], F32, tag="bank", name="latent")
            for t in range(PACK):
                for g in range(PASSES):
                    nc.tensor.matmul_mx(
                        out=latent[:, P * t : P * t + P],
                        lhsT=down_codes[:, g, P * t : P * t + P].bitcast(FP8X4),
                        lhsT_scale=down_scales[:, g, P * t : P * t + P],
                        rhs=x_codes[:, j, g, :].bitcast(FP8X4),
                        rhs_scale=x_scales[:, j, g, :],
                        start=(g == 0),
                        stop=(g == PASSES - 1),
                    )
            latent_grouped = grouped_pool.tile([P, P, PACK], BF16, tag="latent_grouped", name="latent_grouped", align_bytes=64)
            nc.scalar.copy(out=latent_grouped[:], in_=latent[:].rearrange("p (t r) -> p r t", t=PACK))
            return latent_grouped

        def quantise_latent(j, latent_grouped):
            nc.vector.quantize_mx(
                out=latent_codes[:, j, :].bitcast(FP8X4),
                scales=latent_scales[:, j, :],
                in_=latent_grouped[:].rearrange("p r t -> p (r t)"),
            )

        def project_up(codes, scales, n, j, target):
            cols = slice(BANK * n, BANK * n + BANK)
            acc = psum.tile([P, BANK], F32, tag="bank", name="acc")
            nc.tensor.matmul_mx(
                out=acc[:],
                lhsT=latent_codes[:, j, :].bitcast(FP8X4),
                lhsT_scale=latent_scales[:, j, :],
                rhs=codes[:, cols].bitcast(FP8X4),
                rhs_scale=scales[:, cols],
                start=True,
                stop=True,
            )
            nc.scalar.copy(out=target, in_=acc[:].rearrange("p (h d) -> p h d", h=GROUP))

        values_view = out_1.rearrange("b h (p j) d -> p (b h) j d", j=CHUNKS)
        keys_view = out_0.rearrange("b h (p j) d -> p (b h) j d", j=CHUNKS)

        def project_pair_up(codes, scales, q, j0, stage):
            cols = slice(PAIR * HEAD * q, PAIR * HEAD * q + PAIR * HEAD)
            acc = psum.tile([P, BANK], F32, tag="bank", name="acc")
            for c in range(2):
                nc.tensor.matmul_mx(
                    out=acc[:, PAIR * HEAD * c : PAIR * HEAD * c + PAIR * HEAD],
                    lhsT=latent_codes[:, j0 + c, :].bitcast(FP8X4),
                    lhsT_scale=latent_scales[:, j0 + c, :],
                    rhs=codes[:, cols].bitcast(FP8X4),
                    rhs_scale=scales[:, cols],
                    start=True,
                    stop=True,
                )
            nc.scalar.copy(
                out=stage[:, :, j0 : j0 + 2, 0:HEAD], in_=acc[:].rearrange("p (c h d) -> p h c d", c=2, h=PAIR)
            )

        def new_pair_stage(features):
            return stage_pool.tile([P, PAIR, CHUNKS, features], F32, tag="stage", name="stage")

        def store_pair(view, q, stage):
            nc.sync.dma_start(out=view[:, PAIR * q : PAIR * q + PAIR, :, :], in_=stage[:])

        def new_stage(features):
            return stage_pool.tile([P, GROUP, STORE_CHUNKS, features], F32, tag="stage", name="stage")

        def store(view, n, first_chunk, stage, queue=nc.sync):
            queue.dma_start(
                out=view[:, GROUP * n : GROUP * n + GROUP, first_chunk : first_chunk + STORE_CHUNKS, :], in_=stage[:]
            )

        def values(n, j, stage):
            project_up(v_up_codes, v_up_scales, n, j, stage[:, :, j % STORE_CHUNKS, :])

        def rotary(q, j0):
            rot_cols = slice(ROT_COLS * q, ROT_COLS * q + ROT_COLS)
            acc_r = psum.tile([P, BANK], F32, tag="bank", name="acc_r")
            for c in range(ROT_CHUNKS):
                for g in range(PASSES):
                    nc.tensor.matmul_mx(
                        out=acc_r[:, ROT_COLS * c : ROT_COLS * c + ROT_COLS],
                        lhsT=x_codes[:, j0 + c, g, :].bitcast(FP8X4),
                        lhsT_scale=x_scales[:, j0 + c, g, :],
                        rhs=rope_codes[:, g, rot_cols].bitcast(FP8X4),
                        rhs_scale=rope_scales[:, g, rot_cols],
                        start=(g == 0),
                        stop=(g == PASSES - 1),
                    )
            return acc_r

        def rotate(acc_r, j0, stage):
            chunks = slice(j0, j0 + ROT_CHUNKS)
            by_feature = acc_r[:].rearrange("p (c h f) -> p c h f", c=ROT_CHUNKS, h=PAIR)
            by_pair = acc_r[:].rearrange("p (c h i e) -> p c h i e", c=ROT_CHUNKS, h=PAIR, e=2)
            with_cos = rot_pool.tile([P, ROT_CHUNKS, PAIR, PAIRS, 2], F32, tag="with_cos", name="with_cos")
            nc.vector.tensor_tensor(
                out=with_cos[:].rearrange("p c h i e -> p c h (i e)"),
                in0=by_feature,
                in1=cos_twice[:, chunks, :, :].rearrange("p c i e -> p c (i e)").unsqueeze(2).to_broadcast([P, ROT_CHUNKS, PAIR, ROT]),
                op=MULT,
            )
            with_sin = rot_pool.tile([P, ROT_CHUNKS, PAIR, PAIRS, 2], F32, tag="with_sin", name="with_sin")
            nc.vector.tensor_tensor(
                out=with_sin[:],
                in0=by_pair[:, :, :, :, ::-1],
                in1=sin_signed[:, chunks, :, :].unsqueeze(2).to_broadcast([P, ROT_CHUNKS, PAIR, PAIRS, 2]),
                op=MULT,
            )
            nc.gpsimd.tensor_tensor(
                out=stage[:, :, chunks, HEAD : HEAD + ROT].rearrange("p h c (i e) -> p c h i e", e=2),
                in0=with_cos[:],
                in1=with_sin[:],
                op=ADD,
            )

        prepare_down(0)
        prepare_down(1)

        early_stages = {}

        def project_pair(j0):
            return [project_down(j) for j in (j0, j0 + 1)]

        def quantise_pair(j0, tiles):
            for c in range(2):
                quantise_latent(j0 + c, tiles[c])

        def early_values(n, j):
            if j % STORE_CHUNKS == 0:
                early_stages[n] = new_stage(HEAD)
            values(n, j, early_stages[n])
            if (j + 1) % STORE_CHUNKS == 0:
                store(values_view, n, j + 1 - STORE_CHUNKS, early_stages[n])

        rope_steps = [prepare_steps([rope_part(g, h) for h in range(2)]) for g in range(2)]
        fillers = [
            prepare_steps(up_halves(v_up_raw, v_up_codes, v_up_scales, 0), second_copy=nc.scalar.copy),
            rope_steps[0],
            rope_steps[1],
            prepare_steps(up_halves(v_up_raw, v_up_codes, v_up_scales, 1)),
        ]
        for j0 in range(0, CHUNKS, 2):
            tiles = [flip(j) for j in (j0, j0 + 1)]
            for c in range(2):
                quantise_x(j0 + c, tiles[c])
            steps = fillers[j0 // 2]
            between = 0 if j0 == 4 else 2
            if j0 >= 2:
                latents = project_pair(j0 - 2)
            for step in steps[:between]:
                step()
            if j0 >= 2:
                quantise_pair(j0 - 2, latents)
            for step in steps[between:]:
                step()
            if j0 >= 4:
                for j in range(STORE_CHUNKS):
                    early_values(j0 // 2 - 2, j)
        latents = project_pair(CHUNKS - 2)
        quantise_pair(CHUNKS - 2, latents)
        for n in range(2):
            for j in range(CHUNKS - 4, CHUNKS):
                early_values(n, j)

        prepare_rope(2)
        prepare_rope(3)
        prepare(up_halves(k_up_raw, k_up_codes, k_up_scales, 0))
        late_steps = prepare_steps(up_halves(k_up_raw, k_up_codes, k_up_scales, 1))

        rotary_steps = [(q, j0) for q in range(PAIRS_OF_HEADS) for j0 in range(0, CHUNKS, ROT_CHUNKS)]
        key_stages = {}

        def next_rotary():
            q, j0 = rotary_steps.pop(0)
            if j0 == 0:
                key_stages[q] = new_pair_stage(HEAD + ROT)
            rotate(rotary(q, j0), j0, key_stages[q])

        for q in range(PAIRS_OF_HEADS // 2, PAIRS_OF_HEADS):
            stage = new_pair_stage(HEAD)
            for j0 in range(0, CHUNKS, 2):
                project_pair_up(v_up_codes, v_up_scales, q, j0, stage)
                if (q, j0) in ((PAIRS_OF_HEADS - 2, CHUNKS - 2), (PAIRS_OF_HEADS - 1, CHUNKS // 2 - 2)):
                    next_rotary()
            store_pair(values_view, q, stage)

        for q in range(PAIRS_OF_HEADS):
            for j0 in range(0, CHUNKS, 2):
                project_pair_up(k_up_codes, k_up_scales, q, j0, key_stages[q])
                if j0 % 4 == 2 and rotary_steps:
                    next_rotary()
            if late_steps:
                late_steps.pop(0)()
            store_pair(keys_view, q, key_stages[q])
